import numpy as np
import ml_dtypes


def mxq(x, axis, fmt="e4m3"):
    dtype, down = {"e4m3": (ml_dtypes.float8_e4m3fn, 7), "e5m2": (ml_dtypes.float8_e5m2, 14)}[fmt]
    v = np.moveaxis(np.asarray(x, np.float32).astype(ml_dtypes.bfloat16).astype(np.float64), axis, -1)
    blocks = v.reshape(v.shape[:-1] + (-1, 32))
    amax = np.abs(blocks).max(-1, keepdims=True)
    byte = np.maximum(np.where(amax > 0, np.frexp(amax)[1] - 1 + 127, 0) - down, 1)
    scale = np.exp2(byte - 127.0)
    codes = (blocks / scale).astype(np.float32).astype(dtype).astype(np.float64)
    return np.moveaxis((codes * scale).reshape(v.shape), -1, axis)


WIDE = False


def mx_kscale(k):
    if not WIDE:
        return np.ones(k)
    levels = np.array([10, -10, 5, -5, 0])
    a = np.random.permutation(np.resize(levels, k // 512 * 4)).reshape(k // 512, 4)
    idx = np.arange(k)
    return np.exp2(a[idx // 512, idx % 128 // 32])


BF16 = ml_dtypes.bfloat16


def bf(x):
    return np.asarray(x, np.float32).astype(BF16)


def f64(x):
    return np.asarray(x).astype(np.float64)


B, J, C, K, H = 8, 128, 512, 4, 256
KJ = K * J
EPS = 1e-5


def layernorm(v, g, b):
    m = v.mean(-1, keepdims=True)
    var = v.var(-1, keepdims=True)
    return (v - m) / np.sqrt(var + EPS) * g + b


def gcn(xin, adj, spatial_adj, conv_w, conv_b, s_ctx):
    h = (mxq(xin, 2, "e4m3") @ mxq(conv_w, 1, "e4m3").T) + conv_b
    h = h.reshape(B, J, K, C).transpose(0, 2, 1, 3).reshape(B, KJ, C)
    sadj = np.broadcast_to(spatial_adj[None], (B, K - 1, J, J))
    adj4 = np.concatenate([adj * s_ctx, sadj], axis=1).reshape(B, KJ, J)
    return mxq(adj4, 1, "e4m3").transpose(0, 2, 1) @ mxq(h, 1, "e4m3")


def setup_inputs():
    s = mx_kscale(C)
    t = np.sort(mx_kscale(KJ))[np.arange(K) * (KJ - 1) // (K - 1)]
    tw = np.repeat(t, C)
    a = 2.0 / np.sqrt(KJ)
    return {"g1": bf(np.random.standard_normal((B, J, C)) * 0.9 * s),
            "res1": bf(np.random.standard_normal((B, J, C))),
            "adj": bf(np.random.random((B, 1, J, J)) * a / t[0]),
            "spatial_adj": bf(np.random.random((K - 1, J, J)) * a / t[1:, None, None]),
            "conv2_w": bf(np.random.standard_normal((K * C, C)) / np.sqrt(C) / s[None, :] * tw[:, None]),
            "conv2_b": bf(np.random.standard_normal(K * C) * 0.05 * tw),
            "s2": bf(1.5 + 0.1 * np.random.standard_normal(1)),
            "norm2_g": bf(1.0 + 0.1 * np.random.standard_normal(C)),
            "norm2_b": bf(0.1 * np.random.standard_normal(C))}


def reference(g1, res1, adj, spatial_adj, conv2_w, conv2_b, s2, norm2_g, norm2_b):
    g2 = gcn(f64(g1), f64(adj), f64(spatial_adj), f64(conv2_w), f64(conv2_b), f64(s2))
    x2 = f64(res1) + g2
    xn = layernorm(x2, f64(norm2_g), f64(norm2_b))
    return x2, xn

@@ -1,0 +1,251 @@
+from contextlib import ExitStack
+
+import concourse.mybir as mybir
+from concourse.masks import make_identity
+
+F32 = mybir.dt.float32
+BF16 = mybir.dt.bfloat16
+U32 = mybir.dt.uint32
+U8 = mybir.dt.uint8
+FP8X4 = mybir.dt.float8_e4m3fn_x4
+ACT = mybir.ActivationFunctionType
+ALU = mybir.AluOpType
+
+P = 128
+PACK = 4
+B = 8
+J = 128
+C = 512
+K = 4
+R = J // PACK
+CHUNKS = C // P
+GROUP = 4
+N_GROUPS = B // GROUP
+HALF = C // 2
+WORDS = C // 2
+EPS = 1e-5
+
+FLOPS = 2 * B * J * C * K * C + 2 * B * J * K * J * C
+
+
+def tile_block_attention_guide_pb_kernel(
+    tc, g1, res1, adj, spatial_adj, conv2_w, conv2_b, s2, norm2_g, norm2_b, out_0, out_1
+):
+    nc = tc.nc
+    with ExitStack() as ctx:
+        keep = ctx.enter_context(tc.tile_pool(name="keep", bufs=1))
+        per_group = ctx.enter_context(tc.tile_pool(name="per_group", bufs=N_GROUPS))
+        per_sample = ctx.enter_context(tc.tile_pool(name="per_sample", bufs=3))
+        psum_f32 = ctx.enter_context(tc.psum_pool(name="psum_f32", bufs=3))
+        psum_bf16 = ctx.enter_context(tc.psum_pool(name="psum_bf16", bufs=3))
+        psum_out = ctx.enter_context(tc.psum_pool(name="psum_out", bufs=2))
+
+        g1_sb = keep.tile([P, B, C], BF16)
+        w_sb = keep.tile([P, CHUNKS, K, C], BF16)
+        res1_sb = keep.tile([P, B, C], BF16)
+        w_by_chunk = conv2_w.rearrange("(k q p) c -> q p k c", k=K, q=CHUNKS)
+        nc.sync.dma_start(out=g1_sb[:, 0:GROUP], in_=g1[0:GROUP].rearrange("b j c -> j b c"))
+        for q in range(CHUNKS):
+            nc.sync.dma_start(out=w_sb[:, q], in_=w_by_chunk[q])
+        nc.sync.dma_start(out=g1_sb[:, GROUP:B], in_=g1[GROUP:B].rearrange("b j c -> j b c"))
+        nc.sync.dma_start(out=res1_sb[:], in_=res1.rearrange("b w c -> w b c"))
+
+        bias_rows = keep.tile([P, P], BF16)
+        nc.vector.memset(bias_rows[:], 0.0)
+        nc.scalar.dma_start(out=bias_rows[0 : K * CHUNKS, :], in_=conv2_b.rearrange("(i p) -> i p", p=P))
+        s2_all = keep.tile([P, 1], BF16)
+        nc.scalar.dma_start(out=s2_all[:], in_=s2.partition_broadcast(P))
+        a_raw = keep.tile([P, B, PACK * J], BF16)
+        nc.scalar.dma_start(out=a_raw[0:R], in_=adj.rearrange("b o (r t) w -> r (b o) (t w)", t=PACK))
+        nc.scalar.dma_start(
+            out=a_raw[R:P],
+            in_=spatial_adj.rearrange("k (r t) w -> (k r) (t w)", t=PACK).unsqueeze(1).to_broadcast([P - R, B, PACK * J]),
+        )
+        gamma = keep.tile([P, C], BF16)
+        beta = keep.tile([P, C], BF16)
+        nc.scalar.dma_start(out=gamma[:], in_=norm2_g.partition_broadcast(P))
+        nc.scalar.dma_start(out=beta[:], in_=norm2_b.partition_broadcast(P))
+
+        eps = keep.tile([P, 1], F32)
+        nc.vector.memset(eps[:], EPS)
+        table_warm = keep.tile([P, 1], F32)
+        nc.scalar.activation(out=table_warm[:], in_=eps[:], func=ACT.Sqrt)
+        ident_f32 = keep.tile([P, P], F32)
+        make_identity(nc, ident_f32[:])
+        ident_bf16 = keep.tile([P, P], BF16)
+        make_identity(nc, ident_bf16[:])
+
+        bias_ps = psum_bf16.tile([P, P], BF16, tag="bank")
+        nc.tensor.transpose(bias_ps[:], bias_rows[:], ident_bf16[:])
+        bias_col = keep.tile([P, K * CHUNKS], F32)
+        nc.vector.tensor_copy(out=bias_col[:], in_=bias_ps[:, 0 : K * CHUNKS])
+
+        gain = keep.tile([P, 1], F32)
+        nc.vector.memset(gain[:], 1.0)
+        nc.vector.tensor_copy(out=gain[0:R, :], in_=s2_all[0:R, :])
+
+        g1_grouped = keep.tile([P, B, J, PACK], BF16, align_bytes=64)
+        g1_codes = keep.tile([P, N_GROUPS, GROUP * J], U32, align_bytes=64)
+        g1_scales = keep.tile([P, N_GROUPS, GROUP * J], U8, align_bytes=64)
+        w_grouped = keep.tile([P, CHUNKS, K, P, PACK], BF16, align_bytes=64)
+        w_codes = keep.tile([P, CHUNKS, K * P], U32, align_bytes=64)
+        w_scales = keep.tile([P, CHUNKS, K * P], U8, align_bytes=64)
+        a_grouped = keep.tile([P, B, J, PACK], BF16, align_bytes=64)
+        a_codes = keep.tile([P, B * J], U32, align_bytes=64)
+        a_scales = keep.tile([P, B * J], U8, align_bytes=64)
+
+        def transpose_words(bank_part, rows):
+            words = rows.bitcast(F32)
+            for u in range(WORDS // P):
+                nc.tensor.transpose(bank_part[:, u, :], words[:, u * P : (u + 1) * P], ident_f32[:])
+
+        def prepare_g1(g):
+            for pair in range(GROUP // 2):
+                bank = psum_f32.tile([P, 2, WORDS // P, P], F32, tag="bank")
+                for i in range(2):
+                    transpose_words(bank[:, i], g1_sb[:, g * GROUP + 2 * pair + i, :])
+                for i in range(2):
+                    b = g * GROUP + 2 * pair + i
+                    nc.vector.tensor_copy(
+                        out=g1_grouped[:, b]
+                        .rearrange("p n e -> p (n e)")
+                        .bitcast(F32)
+                        .rearrange("p (t r u) -> p t r u", t=PACK, r=R),
+                        in_=bank[:, i].rearrange("p u (r t) -> p t r u", t=PACK),
+                    )
+            nc.vector.quantize_mx(
+                out=g1_codes[:, g, :].bitcast(FP8X4),
+                scales=g1_scales[:, g, :],
+                in_=g1_grouped[:, g * GROUP : (g + 1) * GROUP].rearrange("p b n e -> p (b n e)"),
+            )
+
+        def prepare_w(q):
+            for pair in range(K // 2):
+                bank = psum_f32.tile([P, 2, WORDS // P, P], F32, tag="bank")
+                for i in range(2):
+                    transpose_words(bank[:, i], w_sb[:, q, 2 * pair + i, :])
+                out_words = (
+                    w_grouped[:, q, 2 * pair : 2 * pair + 2]
+                    .rearrange("p k m e -> p (k m e)")
+                    .bitcast(F32)
+                    .rearrange("p (k m u) -> p k m u", k=2, m=P)
+                )
+                in_words = bank[:].rearrange("p k u m -> p k m u")
+                if pair == 0:
+                    nc.vector.tensor_copy(out=out_words, in_=in_words)
+                else:
+                    nc.scalar.copy(out=out_words, in_=in_words)
+            nc.vector.quantize_mx(
+                out=w_codes[:, q, :].bitcast(FP8X4),
+                scales=w_scales[:, q, :],
+                in_=w_grouped[:, q].rearrange("p k m e -> p (k m e)"),
+            )
+
+        def prepare_a():
+            for g in range(N_GROUPS):
+                samples = slice(g * GROUP, (g + 1) * GROUP)
+                nc.vector.tensor_scalar(
+                    out=a_grouped[:, samples],
+                    in0=a_raw[:, samples].rearrange("p b (t w) -> p b w t", t=PACK),
+                    scalar1=gain[:, 0:1],
+                    scalar2=None,
+                    op0=ALU.mult,
+                )
+            nc.vector.quantize_mx(
+                out=a_codes[:].bitcast(FP8X4),
+                scales=a_scales[:],
+                in_=a_grouped[:].rearrange("p b w t -> p (b w t)"),
+            )
+
+        def step1(g, q, h_t):
+            for k in range(K):
+                acc = psum_f32.tile([P, GROUP * J], F32, tag="bank")
+                nc.tensor.matmul_mx(
+                    out=acc[:],
+                    lhsT=w_codes[:, q, k * P : (k + 1) * P].bitcast(FP8X4),
+                    lhsT_scale=w_scales[:, q, k * P : (k + 1) * P],
+                    rhs=g1_codes[:, g, :].bitcast(FP8X4),
+                    rhs_scale=g1_scales[:, g, :],
+                    start=True,
+                    stop=True,
+                )
+                nc.scalar.activation(
+                    out=h_t[:, :, q, :, k, :],
+                    in_=acc[:].rearrange("p (b t r) -> p b t r", b=GROUP, t=PACK),
+                    func=ACT.Identity,
+                    bias=bias_col[:, k * CHUNKS + q : k * CHUNKS + q + 1],
+                    scale=1.0,
+                )
+
+        def transpose_h(h_t, i, half, h_grouped, on_scalar):
+            bank = psum_bf16.tile([P, 2, PACK, P], BF16, tag="bank")
+            for qq in range(2):
+                for t in range(PACK):
+                    nc.tensor.transpose(
+                        bank[:, qq, t, :], h_t[:, i, 2 * half + qq, t].rearrange("p k r -> p (k r)"), ident_bf16[:]
+                    )
+            out_view = h_grouped[:, half * HALF : (half + 1) * HALF, :].rearrange("p (q c) t -> p q c t", q=2)
+            in_view = bank[:].rearrange("p q t c -> p q c t")
+            if on_scalar:
+                nc.scalar.copy(out=out_view, in_=in_view)
+            else:
+                nc.vector.tensor_copy(out=out_view, in_=in_view)
+
+        def step2_and_norm(b, h_grouped):
+            h_codes = per_sample.tile([P, C], U32, align_bytes=64)
+            h_scales = per_sample.tile([P, C], U8, align_bytes=64)
+            nc.vector.quantize_mx(
+                out=h_codes[:].bitcast(FP8X4), scales=h_scales[:], in_=h_grouped[:].rearrange("p c t -> p (c t)")
+            )
+            g2 = psum_out.tile([P, C], F32)
+            nc.tensor.matmul_mx(
+                out=g2[:],
+                lhsT=a_codes[:, b * J : (b + 1) * J].bitcast(FP8X4),
+                lhsT_scale=a_scales[:, b * J : (b + 1) * J],
+                rhs=h_codes[:].bitcast(FP8X4),
+                rhs_scale=h_scales[:],
+                start=True,
+                stop=True,
+            )
+            x2 = per_sample.tile([P, C], F32)
+            nc.vector.tensor_tensor(out=x2[:], in0=g2[:], in1=res1_sb[:, b, :], op=ALU.add)
+            nc.sync.dma_start(out=out_0[b], in_=x2[:])
+
+            stats = per_sample.tile([P, 6], F32)
+            nc.vector.bn_stats(out=stats[:], in_=x2[:])
+            mean_var = per_sample.tile([P, 2], F32)
+            nc.vector.bn_aggr(out=mean_var[:], in_=stats[:])
+            std = per_sample.tile([P, 1], F32)
+            nc.scalar.activation(out=std[:], in_=mean_var[:, 1:2], func=ACT.Sqrt, bias=eps[:, 0:1], scale=1.0)
+            rstd = per_sample.tile([P, 1], F32)
+            nc.vector.reciprocal(out=rstd[:], in_=std[:])
+            shift = per_sample.tile([P, 1], F32)
+            nc.vector.tensor_scalar(
+                out=shift[:], in0=mean_var[:, 0:1], scalar1=rstd[:, 0:1], scalar2=-1.0, op0=ALU.mult, op1=ALU.mult
+            )
+            centred = per_sample.tile([P, C], F32)
+            nc.scalar.activation(out=centred[:], in_=x2[:], func=ACT.Identity, bias=shift[:, 0:1], scale=rstd[:, 0:1])
+            scaled = per_sample.tile([P, C], F32)
+            nc.gpsimd.tensor_tensor(out=scaled[:], in0=centred[:], in1=gamma[:], op=ALU.mult)
+            xn = per_sample.tile([P, C], F32)
+            nc.gpsimd.tensor_tensor(out=xn[:], in0=scaled[:], in1=beta[:], op=ALU.add)
+            nc.sync.dma_start(out=out_1[b], in_=xn[:])
+
+        for g in range(N_GROUPS):
+            prepare_g1(g)
+            h_t = per_group.tile([P, GROUP, CHUNKS, PACK, K, R], BF16)
+            h_grouped = [
+                per_group.tile([P, C, PACK], BF16, align_bytes=64, name="h_grouped_%d" % i) for i in range(GROUP)
+            ]
+            for q in range(CHUNKS):
+                if g == 0:
+                    prepare_w(q)
+                step1(g, q, h_t)
+                if q == 1:
+                    for i in range(GROUP):
+                        transpose_h(h_t, i, 0, h_grouped[i], on_scalar=False)
+            if g == 0:
+                prepare_a()
+            for i in range(GROUP):
+                transpose_h(h_t, i, 1, h_grouped[i], on_scalar=(i % 2 == 1))
+                step2_and_norm(g * GROUP + i, h_grouped[i])

@@ -21,8 +21,6 @@ R = J // PACK
 CHUNKS = C // P
 GROUP = 4
 N_GROUPS = B // GROUP
-HALF = C // 2
-WORDS = C // 2
 EPS = 1e-5
 
 FLOPS = 2 * B * J * C * K * C + 2 * B * J * K * J * C
@@ -33,56 +31,53 @@ def tile_block_attention_guide_pb_kernel(
 ):
     nc = tc.nc
     with ExitStack() as ctx:
+        ctx.enter_context(tc.manual_schedule())
         keep = ctx.enter_context(tc.tile_pool(name="keep", bufs=1))
-        per_group = ctx.enter_context(tc.tile_pool(name="per_group", bufs=N_GROUPS))
+        per_group = ctx.enter_context(tc.tile_pool(name="per_group", bufs=2))
         per_sample = ctx.enter_context(tc.tile_pool(name="per_sample", bufs=3))
-        psum_f32 = ctx.enter_context(tc.psum_pool(name="psum_f32", bufs=3))
-        psum_bf16 = ctx.enter_context(tc.psum_pool(name="psum_bf16", bufs=3))
-        psum_out = ctx.enter_context(tc.psum_pool(name="psum_out", bufs=2))
+        psum_tr = ctx.enter_context(tc.psum_pool(name="psum_tr", bufs=4))
+        psum_s1 = ctx.enter_context(tc.psum_pool(name="psum_s1", bufs=3))
+        psum_s2 = ctx.enter_context(tc.psum_pool(name="psum_s2", bufs=1))
 
         g1_sb = keep.tile([P, B, C], BF16)
         w_sb = keep.tile([P, CHUNKS, K, C], BF16)
         res1_sb = keep.tile([P, B, C], BF16)
         w_by_chunk = conv2_w.rearrange("(k q p) c -> q p k c", k=K, q=CHUNKS)
         nc.sync.dma_start(out=g1_sb[:, 0:GROUP], in_=g1[0:GROUP].rearrange("b j c -> j b c"))
-        for q in range(CHUNKS):
-            nc.sync.dma_start(out=w_sb[:, q], in_=w_by_chunk[q])
-        nc.sync.dma_start(out=g1_sb[:, GROUP:B], in_=g1[GROUP:B].rearrange("b j c -> j b c"))
-        nc.sync.dma_start(out=res1_sb[:], in_=res1.rearrange("b w c -> w b c"))
-
+        nc.sync.dma_start(out=w_sb[:, 0], in_=w_by_chunk[0])
         bias_rows = keep.tile([P, P], BF16)
         nc.vector.memset(bias_rows[:], 0.0)
-        nc.scalar.dma_start(out=bias_rows[0 : K * CHUNKS, :], in_=conv2_b.rearrange("(i p) -> i p", p=P))
+        nc.sync.dma_start(out=bias_rows[0 : K * CHUNKS, :], in_=conv2_b.rearrange("(i p) -> i p", p=P))
+        for q in range(1, CHUNKS):
+            nc.sync.dma_start(out=w_sb[:, q], in_=w_by_chunk[q])
+        nc.sync.dma_start(out=g1_sb[:, GROUP:B], in_=g1[GROUP:B].rearrange("b j c -> j b c"))
         s2_all = keep.tile([P, 1], BF16)
-        nc.scalar.dma_start(out=s2_all[:], in_=s2.partition_broadcast(P))
+        nc.sync.dma_start(out=s2_all[:], in_=s2.partition_broadcast(P))
         a_raw = keep.tile([P, B, PACK * J], BF16)
-        nc.scalar.dma_start(out=a_raw[0:R], in_=adj.rearrange("b o (r t) w -> r (b o) (t w)", t=PACK))
-        nc.scalar.dma_start(
+        nc.sync.dma_start(out=a_raw[0:R], in_=adj.rearrange("b o (r t) w -> r (b o) (t w)", t=PACK))
+        nc.sync.dma_start(
             out=a_raw[R:P],
             in_=spatial_adj.rearrange("k (r t) w -> (k r) (t w)", t=PACK).unsqueeze(1).to_broadcast([P - R, B, PACK * J]),
         )
+        nc.sync.dma_start(out=res1_sb[:], in_=res1.rearrange("b w c -> w b c"))
         gamma = keep.tile([P, C], BF16)
         beta = keep.tile([P, C], BF16)
-        nc.scalar.dma_start(out=gamma[:], in_=norm2_g.partition_broadcast(P))
-        nc.scalar.dma_start(out=beta[:], in_=norm2_b.partition_broadcast(P))
+        nc.sync.dma_start(out=gamma[:], in_=norm2_g.partition_broadcast(P))
+        nc.sync.dma_start(out=beta[:], in_=norm2_b.partition_broadcast(P))
 
-        eps = keep.tile([P, 1], F32)
-        nc.vector.memset(eps[:], EPS)
-        table_warm = keep.tile([P, 1], F32)
-        nc.scalar.activation(out=table_warm[:], in_=eps[:], func=ACT.Sqrt)
         ident_f32 = keep.tile([P, P], F32)
         make_identity(nc, ident_f32[:])
         ident_bf16 = keep.tile([P, P], BF16)
         make_identity(nc, ident_bf16[:])
-
-        bias_ps = psum_bf16.tile([P, P], BF16, tag="bank")
-        nc.tensor.transpose(bias_ps[:], bias_rows[:], ident_bf16[:])
-        bias_col = keep.tile([P, K * CHUNKS], F32)
-        nc.vector.tensor_copy(out=bias_col[:], in_=bias_ps[:, 0 : K * CHUNKS])
-
+        joint_order = keep.tile([P, P], F32)
+        nc.vector.tensor_copy(
+            out=joint_order[:].rearrange("p (a r e) -> p a r e", a=2, e=2),
+            in_=ident_f32[:].rearrange("p (r a e) -> p a r e", a=2, e=2),
+        )
+        minus_half = keep.tile([P, 1], F32)
+        nc.vector.memset(minus_half[:], -0.5)
         gain = keep.tile([P, 1], F32)
         nc.vector.memset(gain[:], 1.0)
-        nc.vector.tensor_copy(out=gain[0:R, :], in_=s2_all[0:R, :])
 
         g1_grouped = keep.tile([P, B, J, PACK], BF16, align_bytes=64)
         g1_codes = keep.tile([P, N_GROUPS, GROUP * J], U32, align_bytes=64)
@@ -91,50 +86,47 @@ def tile_block_attention_guide_pb_kernel(
         w_codes = keep.tile([P, CHUNKS, K * P], U32, align_bytes=64)
         w_scales = keep.tile([P, CHUNKS, K * P], U8, align_bytes=64)
         a_grouped = keep.tile([P, B, J, PACK], BF16, align_bytes=64)
-        a_codes = keep.tile([P, B * J], U32, align_bytes=64)
-        a_scales = keep.tile([P, B * J], U8, align_bytes=64)
+        a_codes = keep.tile([P, B, J], U32, align_bytes=64)
+        a_scales = keep.tile([P, B, J], U8, align_bytes=64)
 
-        def transpose_words(bank_part, rows):
-            words = rows.bitcast(F32)
-            for u in range(WORDS // P):
-                nc.tensor.transpose(bank_part[:, u, :], words[:, u * P : (u + 1) * P], ident_f32[:])
+        def transpose_two(rows_0, rows_1, selector):
+            bank = psum_tr.tile([P, 2, 2, P], F32, tag="bank")
+            for i, rows in enumerate((rows_0, rows_1)):
+                words = rows.bitcast(F32)
+                for u in range(2):
+                    nc.tensor.transpose(bank[:, i, u, :], words[:, u * P : (u + 1) * P], selector[:])
+            return bank
 
-        def prepare_g1(g):
+        def group_two(on_scalar, grouped, bank):
+            out_words = (
+                grouped.rearrange("p i n e -> p (i n e)").bitcast(F32).rearrange("p (i n u) -> p i n u", i=2, u=2)
+            )
+            in_words = bank[:].rearrange("p i u n -> p i n u")
+            if on_scalar:
+                nc.scalar.copy(out=out_words, in_=in_words)
+            else:
+                nc.vector.tensor_copy(out=out_words, in_=in_words)
+
+        def spread_g1(g):
             for pair in range(GROUP // 2):
-                bank = psum_f32.tile([P, 2, WORDS // P, P], F32, tag="bank")
-                for i in range(2):
-                    transpose_words(bank[:, i], g1_sb[:, g * GROUP + 2 * pair + i, :])
-                for i in range(2):
-                    b = g * GROUP + 2 * pair + i
-                    nc.vector.tensor_copy(
-                        out=g1_grouped[:, b]
-                        .rearrange("p n e -> p (n e)")
-                        .bitcast(F32)
-                        .rearrange("p (t r u) -> p t r u", t=PACK, r=R),
-                        in_=bank[:, i].rearrange("p u (r t) -> p t r u", t=PACK),
-                    )
+                b = g * GROUP + 2 * pair
+                bank = transpose_two(g1_sb[:, b, :], g1_sb[:, b + 1, :], joint_order)
+                group_two(pair % 2 == 1, g1_grouped[:, b : b + 2], bank)
+
+        def quantise_g1(g):
             nc.vector.quantize_mx(
                 out=g1_codes[:, g, :].bitcast(FP8X4),
                 scales=g1_scales[:, g, :],
                 in_=g1_grouped[:, g * GROUP : (g + 1) * GROUP].rearrange("p b n e -> p (b n e)"),
             )
 
-        def prepare_w(q):
+        def spread_w(q):
             for pair in range(K // 2):
-                bank = psum_f32.tile([P, 2, WORDS // P, P], F32, tag="bank")
-                for i in range(2):
-                    transpose_words(bank[:, i], w_sb[:, q, 2 * pair + i, :])
-                out_words = (
-                    w_grouped[:, q, 2 * pair : 2 * pair + 2]
-                    .rearrange("p k m e -> p (k m e)")
-                    .bitcast(F32)
-                    .rearrange("p (k m u) -> p k m u", k=2, m=P)
-                )
-                in_words = bank[:].rearrange("p k u m -> p k m u")
-                if pair == 0:
-                    nc.vector.tensor_copy(out=out_words, in_=in_words)
-                else:
-                    nc.scalar.copy(out=out_words, in_=in_words)
+                k = 2 * pair
+                bank = transpose_two(w_sb[:, q, k, :], w_sb[:, q, k + 1, :], ident_f32)
+                group_two(pair % 2 == 1, w_grouped[:, q, k : k + 2], bank)
+
+        def quantise_w(q):
             nc.vector.quantize_mx(
                 out=w_codes[:, q, :].bitcast(FP8X4),
                 scales=w_scales[:, q, :],
@@ -142,8 +134,9 @@ def tile_block_attention_guide_pb_kernel(
             )
 
         def prepare_a():
-            for g in range(N_GROUPS):
-                samples = slice(g * GROUP, (g + 1) * GROUP)
+            nc.vector.tensor_copy(out=gain[0:R, :], in_=s2_all[0:R, :])
+            halves = [slice(half * B // 2, (half + 1) * B // 2) for half in range(2)]
+            for samples in halves:
                 nc.vector.tensor_scalar(
                     out=a_grouped[:, samples],
                     in0=a_raw[:, samples].rearrange("p b (t w) -> p b w t", t=PACK),
@@ -151,15 +144,21 @@ def tile_block_attention_guide_pb_kernel(
                     scalar2=None,
                     op0=ALU.mult,
                 )
-            nc.vector.quantize_mx(
-                out=a_codes[:].bitcast(FP8X4),
-                scales=a_scales[:],
-                in_=a_grouped[:].rearrange("p b w t -> p (b w t)"),
-            )
+            for samples in halves:
+                nc.vector.quantize_mx(
+                    out=a_codes[:, samples, :].rearrange("p b w -> p (b w)").bitcast(FP8X4),
+                    scales=a_scales[:, samples, :].rearrange("p b w -> p (b w)"),
+                    in_=a_grouped[:, samples].rearrange("p b w t -> p (b w t)"),
+                )
 
-        def step1(g, q, h_t):
+        h_t = {}
+
+        def step1(g, q):
+            if q == 0:
+                h_t_new = per_group.tile([P, GROUP, CHUNKS, C], BF16, tag="h_t")
+                h_t[g] = h_t_new
             for k in range(K):
-                acc = psum_f32.tile([P, GROUP * J], F32, tag="bank")
+                acc = psum_s1.tile([P, GROUP * J], F32)
                 nc.tensor.matmul_mx(
                     out=acc[:],
                     lhsT=w_codes[:, q, k * P : (k + 1) * P].bitcast(FP8X4),
@@ -170,82 +169,127 @@ def tile_block_attention_guide_pb_kernel(
                     stop=True,
                 )
                 nc.scalar.activation(
-                    out=h_t[:, :, q, :, k, :],
-                    in_=acc[:].rearrange("p (b t r) -> p b t r", b=GROUP, t=PACK),
+                    out=h_t[g][:, :, q, :].rearrange("p b (a k n) -> p b a k n", a=2, k=K)[:, :, :, k, :],
+                    in_=acc[:].rearrange("p (b a n) -> p b a n", b=GROUP, a=2),
                     func=ACT.Identity,
                     bias=bias_col[:, k * CHUNKS + q : k * CHUNKS + q + 1],
                     scale=1.0,
                 )
 
-        def transpose_h(h_t, i, half, h_grouped, on_scalar):
-            bank = psum_bf16.tile([P, 2, PACK, P], BF16, tag="bank")
-            for qq in range(2):
-                for t in range(PACK):
-                    nc.tensor.transpose(
-                        bank[:, qq, t, :], h_t[:, i, 2 * half + qq, t].rearrange("p k r -> p (k r)"), ident_bf16[:]
-                    )
-            out_view = h_grouped[:, half * HALF : (half + 1) * HALF, :].rearrange("p (q c) t -> p q c t", q=2)
-            in_view = bank[:].rearrange("p q t c -> p q c t")
-            if on_scalar:
-                nc.scalar.copy(out=out_view, in_=in_view)
-            else:
-                nc.vector.tensor_copy(out=out_view, in_=in_view)
+        h_banks = {}
+        h_grouped = {}
+        g2 = {}
+        x2 = {}
+        stats = {}
+        mean_var = {}
+        rstd = {}
+        centred = {}
 
-        def step2_and_norm(b, h_grouped):
+        def transpose_h(b):
+            rows = h_t[b // GROUP][:, b % GROUP]
+            h_banks[b] = [transpose_two(rows[:, 2 * half, :], rows[:, 2 * half + 1, :], ident_f32) for half in range(2)]
+
+        def group_h(b):
+            h_grouped_new = per_sample.tile([P, CHUNKS, P, PACK], BF16, align_bytes=64, tag="h_grouped")
+            h_grouped[b] = h_grouped_new
+            for half in range(2):
+                group_two(True, h_grouped_new[:, 2 * half : 2 * half + 2], h_banks[b][half])
+
+        def step2(b):
             h_codes = per_sample.tile([P, C], U32, align_bytes=64)
             h_scales = per_sample.tile([P, C], U8, align_bytes=64)
             nc.vector.quantize_mx(
-                out=h_codes[:].bitcast(FP8X4), scales=h_scales[:], in_=h_grouped[:].rearrange("p c t -> p (c t)")
+                out=h_codes[:].bitcast(FP8X4), scales=h_scales[:], in_=h_grouped[b][:].rearrange("p q c t -> p (q c t)")
             )
-            g2 = psum_out.tile([P, C], F32)
+            g2_new = psum_s2.tile([P, C], F32, tag="g2")
+            g2[b] = g2_new
             nc.tensor.matmul_mx(
-                out=g2[:],
-                lhsT=a_codes[:, b * J : (b + 1) * J].bitcast(FP8X4),
-                lhsT_scale=a_scales[:, b * J : (b + 1) * J],
+                out=g2_new[:],
+                lhsT=a_codes[:, b, :].bitcast(FP8X4),
+                lhsT_scale=a_scales[:, b, :],
                 rhs=h_codes[:].bitcast(FP8X4),
                 rhs_scale=h_scales[:],
                 start=True,
                 stop=True,
             )
-            x2 = per_sample.tile([P, C], F32)
-            nc.vector.tensor_tensor(out=x2[:], in0=g2[:], in1=res1_sb[:, b, :], op=ALU.add)
-            nc.sync.dma_start(out=out_0[b], in_=x2[:])
 
-            stats = per_sample.tile([P, 6], F32)
-            nc.vector.bn_stats(out=stats[:], in_=x2[:])
-            mean_var = per_sample.tile([P, 2], F32)
-            nc.vector.bn_aggr(out=mean_var[:], in_=stats[:])
-            std = per_sample.tile([P, 1], F32)
-            nc.scalar.activation(out=std[:], in_=mean_var[:, 1:2], func=ACT.Sqrt, bias=eps[:, 0:1], scale=1.0)
-            rstd = per_sample.tile([P, 1], F32)
-            nc.vector.reciprocal(out=rstd[:], in_=std[:])
-            shift = per_sample.tile([P, 1], F32)
-            nc.vector.tensor_scalar(
-                out=shift[:], in0=mean_var[:, 0:1], scalar1=rstd[:, 0:1], scalar2=-1.0, op0=ALU.mult, op1=ALU.mult
+        def residual(b):
+            x2_new = per_sample.tile([P, C], F32, tag="x2")
+            x2[b] = x2_new
+            nc.vector.tensor_tensor(out=x2_new[:], in0=g2[b][:], in1=res1_sb[:, b, :], op=ALU.add)
+            nc.sync.dma_start(out=out_0[b], in_=x2_new[:])
+
+        def statistics(b):
+            stats_new = per_sample.tile([P, 6], F32, tag="stats")
+            stats[b] = stats_new
+            nc.vector.bn_stats(out=stats_new[:], in_=x2[b][:])
+
+        def mean_and_rstd(b):
+            mean_var_new = per_sample.tile([P, 2], F32, tag="mean_var")
+            mean_var[b] = mean_var_new
+            nc.vector.bn_aggr(out=mean_var_new[:], in_=stats[b][:])
+            var_eps = per_sample.tile([P, 1], F32)
+            nc.gpsimd.tensor_scalar(out=var_eps[:], in0=mean_var_new[:, 1:2], scalar1=EPS, scalar2=None, op0=ALU.add)
+            rstd_new = per_sample.tile([P, 1], F32, tag="rstd")
+            rstd[b] = rstd_new
+            nc.gpsimd.tensor_tensor(out=rstd_new[:], in0=var_eps[:], in1=minus_half[:], op=ALU.pow)
+
+        def centre(b):
+            centred_new = per_sample.tile([P, C], F32, tag="centred")
+            centred[b] = centred_new
+            nc.vector.scalar_tensor_tensor(
+                out=centred_new[:], in0=x2[b][:], scalar=mean_var[b][:, 0:1], in1=gamma[:], op0=ALU.subtract, op1=ALU.mult
             )
-            centred = per_sample.tile([P, C], F32)
-            nc.scalar.activation(out=centred[:], in_=x2[:], func=ACT.Identity, bias=shift[:, 0:1], scale=rstd[:, 0:1])
-            scaled = per_sample.tile([P, C], F32)
-            nc.gpsimd.tensor_tensor(out=scaled[:], in0=centred[:], in1=gamma[:], op=ALU.mult)
+
+        def scale_and_shift(b):
             xn = per_sample.tile([P, C], F32)
-            nc.gpsimd.tensor_tensor(out=xn[:], in0=scaled[:], in1=beta[:], op=ALU.add)
+            nc.vector.scalar_tensor_tensor(
+                out=xn[:], in0=centred[b][:], scalar=rstd[b][:, 0:1], in1=beta[:], op0=ALU.mult, op1=ALU.add
+            )
             nc.sync.dma_start(out=out_1[b], in_=xn[:])
 
-        for g in range(N_GROUPS):
-            prepare_g1(g)
-            h_t = per_group.tile([P, GROUP, CHUNKS, PACK, K, R], BF16)
-            h_grouped = [
-                per_group.tile([P, C, PACK], BF16, align_bytes=64, name="h_grouped_%d" % i) for i in range(GROUP)
-            ]
-            for q in range(CHUNKS):
-                if g == 0:
-                    prepare_w(q)
-                step1(g, q, h_t)
-                if q == 1:
-                    for i in range(GROUP):
-                        transpose_h(h_t, i, 0, h_grouped[i], on_scalar=False)
-            if g == 0:
-                prepare_a()
-            for i in range(GROUP):
-                transpose_h(h_t, i, 1, h_grouped[i], on_scalar=(i % 2 == 1))
-                step2_and_norm(g * GROUP + i, h_grouped[i])
+
+        spread_g1(0)
+        spread_w(0)
+        quantise_g1(0)
+        quantise_w(0)
+        spread_w(1)
+        bias_ps = psum_tr.tile([P, P], BF16, tag="bank")
+        nc.tensor.transpose(bias_ps[:], bias_rows[:], ident_bf16[:])
+        bias_col = keep.tile([P, K * CHUNKS], F32)
+        nc.vector.tensor_copy(out=bias_col[:], in_=bias_ps[:, 0 : K * CHUNKS])
+        for q in range(CHUNKS):
+            if q + 1 < CHUNKS:
+                quantise_w(q + 1)
+            if q + 1 == CHUNKS:
+                for g in range(1, N_GROUPS):
+                    quantise_g1(g)
+            step1(0, q)
+            if q + 2 < CHUNKS:
+                spread_w(q + 2)
+            if q + 2 == CHUNKS:
+                for g in range(1, N_GROUPS):
+                    spread_g1(g)
+        prepare_a()
+
+        chunks_a_round = CHUNKS // GROUP
+        transpose_h(0)
+        for b in range(B + 2):
+            if b < B:
+                group_h(b)
+                if b // GROUP + 1 < N_GROUPS:
+                    for q in range((b % GROUP) * chunks_a_round, (b % GROUP + 1) * chunks_a_round):
+                        step1(b // GROUP + 1, q)
+                if b + 1 < B:
+                    transpose_h(b + 1)
+                step2(b)
+            if 0 <= b - 1 < B:
+                residual(b - 1)
+            if 0 <= b - 2:
+                centre(b - 2)
+            if 0 <= b - 1 < B:
+                statistics(b - 1)
+            if 0 <= b - 2:
+                scale_and_shift(b - 2)
+            if 0 <= b - 1 < B:
+                mean_and_rstd(b - 1)

@@ -19,7 +19,7 @@ C = 512
 K = 4
 R = J // PACK
 CHUNKS = C // P
-GROUP = 4
+GROUP = 2
 N_GROUPS = B // GROUP
 EPS = 1e-5
 
@@ -31,7 +31,6 @@ def tile_block_attention_guide_pb_kernel(
 ):
     nc = tc.nc
     with ExitStack() as ctx:
-        ctx.enter_context(tc.manual_schedule())
         keep = ctx.enter_context(tc.tile_pool(name="keep", bufs=1))
         per_group = ctx.enter_context(tc.tile_pool(name="per_group", bufs=2))
         per_sample = ctx.enter_context(tc.tile_pool(name="per_sample", bufs=3))

@@ -19,8 +19,9 @@ C = 512
 K = 4
 R = J // PACK
 CHUNKS = C // P
-GROUP = 2
+GROUP = 4
 N_GROUPS = B // GROUP
+assert N_GROUPS == 2 and GROUP == CHUNKS
 EPS = 1e-5
 
 FLOPS = 2 * B * J * C * K * C + 2 * B * J * K * J * C
@@ -31,11 +32,12 @@ def tile_block_attention_guide_pb_kernel(
 ):
     nc = tc.nc
     with ExitStack() as ctx:
+        ctx.enter_context(tc.manual_schedule())
         keep = ctx.enter_context(tc.tile_pool(name="keep", bufs=1))
         per_group = ctx.enter_context(tc.tile_pool(name="per_group", bufs=2))
         per_sample = ctx.enter_context(tc.tile_pool(name="per_sample", bufs=3))
-        psum_tr = ctx.enter_context(tc.psum_pool(name="psum_tr", bufs=4))
-        psum_s1 = ctx.enter_context(tc.psum_pool(name="psum_s1", bufs=3))
+        psum_tr = ctx.enter_context(tc.psum_pool(name="psum_tr", bufs=3))
+        psum_s1 = ctx.enter_context(tc.psum_pool(name="psum_s1", bufs=K))
         psum_s2 = ctx.enter_context(tc.psum_pool(name="psum_s2", bufs=1))
 
         g1_sb = keep.tile([P, B, C], BF16)
@@ -49,7 +51,6 @@ def tile_block_attention_guide_pb_kernel(
         nc.sync.dma_start(out=bias_rows[0 : K * CHUNKS, :], in_=conv2_b.rearrange("(i p) -> i p", p=P))
         for q in range(1, CHUNKS):
             nc.sync.dma_start(out=w_sb[:, q], in_=w_by_chunk[q])
-        nc.sync.dma_start(out=g1_sb[:, GROUP:B], in_=g1[GROUP:B].rearrange("b j c -> j b c"))
         s2_all = keep.tile([P, 1], BF16)
         nc.sync.dma_start(out=s2_all[:], in_=s2.partition_broadcast(P))
         a_raw = keep.tile([P, B, PACK * J], BF16)
@@ -58,6 +59,7 @@ def tile_block_attention_guide_pb_kernel(
             out=a_raw[R:P],
             in_=spatial_adj.rearrange("k (r t) w -> (k r) (t w)", t=PACK).unsqueeze(1).to_broadcast([P - R, B, PACK * J]),
         )
+        nc.sync.dma_start(out=g1_sb[:, GROUP:B], in_=g1[GROUP:B].rearrange("b j c -> j b c"))
         nc.sync.dma_start(out=res1_sb[:], in_=res1.rearrange("b w c -> w b c"))
         gamma = keep.tile([P, C], BF16)
         beta = keep.tile([P, C], BF16)
@@ -76,7 +78,8 @@ def tile_block_attention_guide_pb_kernel(
         minus_half = keep.tile([P, 1], F32)
         nc.vector.memset(minus_half[:], -0.5)
         gain = keep.tile([P, 1], F32)
-        nc.vector.memset(gain[:], 1.0)
+        nc.gpsimd.memset(gain[:], 1.0)
+        nc.gpsimd.tensor_copy(out=gain[0:R, :], in_=s2_all[0:R, :])
 
         g1_grouped = keep.tile([P, B, J, PACK], BF16, align_bytes=64)
         g1_codes = keep.tile([P, N_GROUPS, GROUP * J], U32, align_bytes=64)
@@ -132,18 +135,19 @@ def tile_block_attention_guide_pb_kernel(
                 in_=w_grouped[:, q].rearrange("p k m e -> p (k m e)"),
             )
 
-        def prepare_a():
-            nc.vector.tensor_copy(out=gain[0:R, :], in_=s2_all[0:R, :])
-            halves = [slice(half * B // 2, (half + 1) * B // 2) for half in range(2)]
-            for samples in halves:
-                nc.vector.tensor_scalar(
-                    out=a_grouped[:, samples],
-                    in0=a_raw[:, samples].rearrange("p b (t w) -> p b w t", t=PACK),
+        def spread_a():
+            for b in range(B):
+                nc.gpsimd.tensor_scalar(
+                    out=a_grouped[:, b],
+                    in0=a_raw[:, b].rearrange("p (t w) -> p w t", t=PACK),
                     scalar1=gain[:, 0:1],
-                    scalar2=None,
+                    scalar2=0.0,
                     op0=ALU.mult,
+                    op1=ALU.add,
                 )
-            for samples in halves:
+
+        def quantise_a():
+            for samples in (slice(0, B // 2), slice(B // 2, B)):
                 nc.vector.quantize_mx(
                     out=a_codes[:, samples, :].rearrange("p b w -> p (b w)").bitcast(FP8X4),
                     scales=a_scales[:, samples, :].rearrange("p b w -> p (b w)"),
@@ -156,6 +160,7 @@ def tile_block_attention_guide_pb_kernel(
             if q == 0:
                 h_t_new = per_group.tile([P, GROUP, CHUNKS, C], BF16, tag="h_t")
                 h_t[g] = h_t_new
+            banks = []
             for k in range(K):
                 acc = psum_s1.tile([P, GROUP * J], F32)
                 nc.tensor.matmul_mx(
@@ -167,13 +172,17 @@ def tile_block_attention_guide_pb_kernel(
                     start=True,
                     stop=True,
                 )
-                nc.scalar.activation(
-                    out=h_t[g][:, :, q, :].rearrange("p b (a k n) -> p b a k n", a=2, k=K)[:, :, :, k, :],
-                    in_=acc[:].rearrange("p (b a n) -> p b a n", b=GROUP, a=2),
-                    func=ACT.Identity,
-                    bias=bias_col[:, k * CHUNKS + q : k * CHUNKS + q + 1],
-                    scale=1.0,
-                )
+                banks.append(acc)
+            return banks
+
+        def add_bias(on_vector, g, q, k, acc):
+            out_view = h_t[g][:, :, q, :].rearrange("p b (a k n) -> p b a k n", a=2, k=K)[:, :, :, k, :]
+            in_view = acc[:].rearrange("p (b a n) -> p b a n", b=GROUP, a=2)
+            bias = bias_col[:, k * CHUNKS + q : k * CHUNKS + q + 1]
+            if on_vector:
+                nc.vector.tensor_scalar(out=out_view, in0=in_view, scalar1=bias, scalar2=None, op0=ALU.add)
+            else:
+                nc.scalar.activation(out=out_view, in_=in_view, func=ACT.Identity, bias=bias, scale=1.0)
 
         h_banks = {}
         h_grouped = {}
@@ -257,38 +266,43 @@ def tile_block_attention_guide_pb_kernel(
         nc.tensor.transpose(bias_ps[:], bias_rows[:], ident_bf16[:])
         bias_col = keep.tile([P, K * CHUNKS], F32)
         nc.vector.tensor_copy(out=bias_col[:], in_=bias_ps[:, 0 : K * CHUNKS])
+        spread_a()
         for q in range(CHUNKS):
+            banks = step1(0, q)
+            for k in range(K):
+                add_bias(k == K - 1, 0, q, k, banks[k])
             if q + 1 < CHUNKS:
                 quantise_w(q + 1)
-            if q + 1 == CHUNKS:
-                for g in range(1, N_GROUPS):
-                    quantise_g1(g)
-            step1(0, q)
             if q + 2 < CHUNKS:
                 spread_w(q + 2)
             if q + 2 == CHUNKS:
-                for g in range(1, N_GROUPS):
-                    spread_g1(g)
-        prepare_a()
+                spread_g1(1)
+        quantise_g1(1)
+        quantise_a()
 
-        chunks_a_round = CHUNKS // GROUP
         transpose_h(0)
         for b in range(B + 2):
+            filling = b < 2
             if b < B:
                 group_h(b)
-                if b // GROUP + 1 < N_GROUPS:
-                    for q in range((b % GROUP) * chunks_a_round, (b % GROUP + 1) * chunks_a_round):
-                        step1(b // GROUP + 1, q)
+                if b < CHUNKS:
+                    banks = step1(1, b)
+                    for k in range(K - 2 if filling else K):
+                        add_bias(False, 1, b, k, banks[k])
                 if b + 1 < B:
                     transpose_h(b + 1)
                 step2(b)
             if 0 <= b - 1 < B:
                 residual(b - 1)
-            if 0 <= b - 2:
+            if filling:
+                add_bias(True, 1, b, K - 2, banks[K - 2])
+            else:
                 centre(b - 2)
             if 0 <= b - 1 < B:
                 statistics(b - 1)
-            if 0 <= b - 2:
+            if filling:
+                add_bias(True, 1, b, K - 1, banks[K - 1])
+            else:
                 scale_and_shift(b - 2)
             if 0 <= b - 1 < B:
                 mean_and_rstd(b - 1)

@@ -21,7 +21,6 @@ R = J // PACK
 CHUNKS = C // P
 GROUP = 4
 N_GROUPS = B // GROUP
-assert N_GROUPS == 2 and GROUP == CHUNKS
 EPS = 1e-5
 
 FLOPS = 2 * B * J * C * K * C + 2 * B * J * K * J * C
@@ -32,12 +31,11 @@ def tile_block_attention_guide_pb_kernel(
 ):
     nc = tc.nc
     with ExitStack() as ctx:
-        ctx.enter_context(tc.manual_schedule())
         keep = ctx.enter_context(tc.tile_pool(name="keep", bufs=1))
         per_group = ctx.enter_context(tc.tile_pool(name="per_group", bufs=2))
         per_sample = ctx.enter_context(tc.tile_pool(name="per_sample", bufs=3))
-        psum_tr = ctx.enter_context(tc.psum_pool(name="psum_tr", bufs=3))
-        psum_s1 = ctx.enter_context(tc.psum_pool(name="psum_s1", bufs=K))
+        psum_tr = ctx.enter_context(tc.psum_pool(name="psum_tr", bufs=4))
+        psum_s1 = ctx.enter_context(tc.psum_pool(name="psum_s1", bufs=3))
         psum_s2 = ctx.enter_context(tc.psum_pool(name="psum_s2", bufs=1))
 
         g1_sb = keep.tile([P, B, C], BF16)
@@ -51,6 +49,7 @@ def tile_block_attention_guide_pb_kernel(
         nc.sync.dma_start(out=bias_rows[0 : K * CHUNKS, :], in_=conv2_b.rearrange("(i p) -> i p", p=P))
         for q in range(1, CHUNKS):
             nc.sync.dma_start(out=w_sb[:, q], in_=w_by_chunk[q])
+        nc.sync.dma_start(out=g1_sb[:, GROUP:B], in_=g1[GROUP:B].rearrange("b j c -> j b c"))
         s2_all = keep.tile([P, 1], BF16)
         nc.sync.dma_start(out=s2_all[:], in_=s2.partition_broadcast(P))
         a_raw = keep.tile([P, B, PACK * J], BF16)
@@ -59,7 +58,6 @@ def tile_block_attention_guide_pb_kernel(
             out=a_raw[R:P],
             in_=spatial_adj.rearrange("k (r t) w -> (k r) (t w)", t=PACK).unsqueeze(1).to_broadcast([P - R, B, PACK * J]),
         )
-        nc.sync.dma_start(out=g1_sb[:, GROUP:B], in_=g1[GROUP:B].rearrange("b j c -> j b c"))
         nc.sync.dma_start(out=res1_sb[:], in_=res1.rearrange("b w c -> w b c"))
         gamma = keep.tile([P, C], BF16)
         beta = keep.tile([P, C], BF16)
@@ -78,8 +76,7 @@ def tile_block_attention_guide_pb_kernel(
         minus_half = keep.tile([P, 1], F32)
         nc.vector.memset(minus_half[:], -0.5)
         gain = keep.tile([P, 1], F32)
-        nc.gpsimd.memset(gain[:], 1.0)
-        nc.gpsimd.tensor_copy(out=gain[0:R, :], in_=s2_all[0:R, :])
+        nc.vector.memset(gain[:], 1.0)
 
         g1_grouped = keep.tile([P, B, J, PACK], BF16, align_bytes=64)
         g1_codes = keep.tile([P, N_GROUPS, GROUP * J], U32, align_bytes=64)
@@ -135,19 +132,18 @@ def tile_block_attention_guide_pb_kernel(
                 in_=w_grouped[:, q].rearrange("p k m e -> p (k m e)"),
             )
 
-        def spread_a():
-            for b in range(B):
-                nc.gpsimd.tensor_scalar(
-                    out=a_grouped[:, b],
-                    in0=a_raw[:, b].rearrange("p (t w) -> p w t", t=PACK),
+        def prepare_a():
+            nc.vector.tensor_copy(out=gain[0:R, :], in_=s2_all[0:R, :])
+            halves = [slice(half * B // 2, (half + 1) * B // 2) for half in range(2)]
+            for samples in halves:
+                nc.vector.tensor_scalar(
+                    out=a_grouped[:, samples],
+                    in0=a_raw[:, samples].rearrange("p b (t w) -> p b w t", t=PACK),
                     scalar1=gain[:, 0:1],
-                    scalar2=0.0,
+                    scalar2=None,
                     op0=ALU.mult,
-                    op1=ALU.add,
                 )
-
-        def quantise_a():
-            for samples in (slice(0, B // 2), slice(B // 2, B)):
+            for samples in halves:
                 nc.vector.quantize_mx(
                     out=a_codes[:, samples, :].rearrange("p b w -> p (b w)").bitcast(FP8X4),
                     scales=a_scales[:, samples, :].rearrange("p b w -> p (b w)"),
@@ -160,7 +156,6 @@ def tile_block_attention_guide_pb_kernel(
             if q == 0:
                 h_t_new = per_group.tile([P, GROUP, CHUNKS, C], BF16, tag="h_t")
                 h_t[g] = h_t_new
-            banks = []
             for k in range(K):
                 acc = psum_s1.tile([P, GROUP * J], F32)
                 nc.tensor.matmul_mx(
@@ -172,17 +167,13 @@ def tile_block_attention_guide_pb_kernel(
                     start=True,
                     stop=True,
                 )
-                banks.append(acc)
-            return banks
-
-        def add_bias(on_vector, g, q, k, acc):
-            out_view = h_t[g][:, :, q, :].rearrange("p b (a k n) -> p b a k n", a=2, k=K)[:, :, :, k, :]
-            in_view = acc[:].rearrange("p (b a n) -> p b a n", b=GROUP, a=2)
-            bias = bias_col[:, k * CHUNKS + q : k * CHUNKS + q + 1]
-            if on_vector:
-                nc.vector.tensor_scalar(out=out_view, in0=in_view, scalar1=bias, scalar2=None, op0=ALU.add)
-            else:
-                nc.scalar.activation(out=out_view, in_=in_view, func=ACT.Identity, bias=bias, scale=1.0)
+                nc.scalar.activation(
+                    out=h_t[g][:, :, q, :].rearrange("p b (a k n) -> p b a k n", a=2, k=K)[:, :, :, k, :],
+                    in_=acc[:].rearrange("p (b a n) -> p b a n", b=GROUP, a=2),
+                    func=ACT.Identity,
+                    bias=bias_col[:, k * CHUNKS + q : k * CHUNKS + q + 1],
+                    scale=1.0,
+                )
 
         h_banks = {}
         h_grouped = {}
@@ -266,43 +257,38 @@ def tile_block_attention_guide_pb_kernel(
         nc.tensor.transpose(bias_ps[:], bias_rows[:], ident_bf16[:])
         bias_col = keep.tile([P, K * CHUNKS], F32)
         nc.vector.tensor_copy(out=bias_col[:], in_=bias_ps[:, 0 : K * CHUNKS])
-        spread_a()
         for q in range(CHUNKS):
-            banks = step1(0, q)
-            for k in range(K):
-                add_bias(k == K - 1, 0, q, k, banks[k])
             if q + 1 < CHUNKS:
                 quantise_w(q + 1)
+            if q + 1 == CHUNKS:
+                for g in range(1, N_GROUPS):
+                    quantise_g1(g)
+            step1(0, q)
             if q + 2 < CHUNKS:
                 spread_w(q + 2)
             if q + 2 == CHUNKS:
-                spread_g1(1)
-        quantise_g1(1)
-        quantise_a()
+                for g in range(1, N_GROUPS):
+                    spread_g1(g)
+        prepare_a()
 
+        chunks_a_round = CHUNKS // GROUP
         transpose_h(0)
         for b in range(B + 2):
-            filling = b < 2
             if b < B:
                 group_h(b)
-                if b < CHUNKS:
-                    banks = step1(1, b)
-                    for k in range(K - 2 if filling else K):
-                        add_bias(False, 1, b, k, banks[k])
+                if b // GROUP + 1 < N_GROUPS:
+                    for q in range((b % GROUP) * chunks_a_round, (b % GROUP + 1) * chunks_a_round):
+                        step1(b // GROUP + 1, q)
                 if b + 1 < B:
                     transpose_h(b + 1)
                 step2(b)
             if 0 <= b - 1 < B:
                 residual(b - 1)
-            if filling:
-                add_bias(True, 1, b, K - 2, banks[K - 2])
-            else:
+            if 0 <= b - 2:
                 centre(b - 2)
             if 0 <= b - 1 < B:
                 statistics(b - 1)
-            if filling:
-                add_bias(True, 1, b, K - 1, banks[K - 1])
-            else:
+            if 0 <= b - 2:
                 scale_and_shift(b - 2)
             if 0 <= b - 1 < B:
                 mean_and_rstd(b - 1)

from contextlib import ExitStack

import concourse.mybir as mybir
from concourse.masks import make_identity

F32 = mybir.dt.float32
BF16 = mybir.dt.bfloat16
U32 = mybir.dt.uint32
U8 = mybir.dt.uint8
FP8X4 = mybir.dt.float8_e4m3fn_x4
ACT = mybir.ActivationFunctionType
ALU = mybir.AluOpType

P = 128
PACK = 4
B = 8
J = 128
C = 512
K = 4
R = J // PACK
CHUNKS = C // P
GROUP = 4
N_GROUPS = B // GROUP
EPS = 1e-5

FLOPS = 2 * B * J * C * K * C + 2 * B * J * K * J * C


def tile_block_attention_guide_pb_kernel(
    tc, g1, res1, adj, spatial_adj, conv2_w, conv2_b, s2, norm2_g, norm2_b, out_0, out_1
):
    nc = tc.nc
    with ExitStack() as ctx:
        keep = ctx.enter_context(tc.tile_pool(name="keep", bufs=1))
        per_group = ctx.enter_context(tc.tile_pool(name="per_group", bufs=2))
        per_sample = ctx.enter_context(tc.tile_pool(name="per_sample", bufs=3))
        psum_tr = ctx.enter_context(tc.psum_pool(name="psum_tr", bufs=4))
        psum_s1 = ctx.enter_context(tc.psum_pool(name="psum_s1", bufs=3))
        psum_s2 = ctx.enter_context(tc.psum_pool(name="psum_s2", bufs=1))

        g1_sb = keep.tile([P, B, C], BF16)
        w_sb = keep.tile([P, CHUNKS, K, C], BF16)
        res1_sb = keep.tile([P, B, C], BF16)
        w_by_chunk = conv2_w.rearrange("(k q p) c -> q p k c", k=K, q=CHUNKS)
        nc.sync.dma_start(out=g1_sb[:, 0:GROUP], in_=g1[0:GROUP].rearrange("b j c -> j b c"))
        nc.sync.dma_start(out=w_sb[:, 0], in_=w_by_chunk[0])
        bias_rows = keep.tile([P, P], BF16)
        nc.vector.memset(bias_rows[:], 0.0)
        nc.sync.dma_start(out=bias_rows[0 : K * CHUNKS, :], in_=conv2_b.rearrange("(i p) -> i p", p=P))
        for q in range(1, CHUNKS):
            nc.sync.dma_start(out=w_sb[:, q], in_=w_by_chunk[q])
        nc.sync.dma_start(out=g1_sb[:, GROUP:B], in_=g1[GROUP:B].rearrange("b j c -> j b c"))
        s2_all = keep.tile([P, 1], BF16)
        nc.sync.dma_start(out=s2_all[:], in_=s2.partition_broadcast(P))
        a_raw = keep.tile([P, B, PACK * J], BF16)
        nc.sync.dma_start(out=a_raw[0:R], in_=adj.rearrange("b o (r t) w -> r (b o) (t w)", t=PACK))
        nc.sync.dma_start(
            out=a_raw[R:P],
            in_=spatial_adj.rearrange("k (r t) w -> (k r) (t w)", t=PACK).unsqueeze(1).to_broadcast([P - R, B, PACK * J]),
        )
        nc.sync.dma_start(out=res1_sb[:], in_=res1.rearrange("b w c -> w b c"))
        gamma = keep.tile([P, C], BF16)
        beta = keep.tile([P, C], BF16)
        nc.sync.dma_start(out=gamma[:], in_=norm2_g.partition_broadcast(P))
        nc.sync.dma_start(out=beta[:], in_=norm2_b.partition_broadcast(P))

        ident_f32 = keep.tile([P, P], F32)
        make_identity(nc, ident_f32[:])
        ident_bf16 = keep.tile([P, P], BF16)
        make_identity(nc, ident_bf16[:])
        joint_order = keep.tile([P, P], F32)
        nc.vector.tensor_copy(
            out=joint_order[:].rearrange("p (a r e) -> p a r e", a=2, e=2),
            in_=ident_f32[:].rearrange("p (r a e) -> p a r e", a=2, e=2),
        )
        minus_half = keep.tile([P, 1], F32)
        nc.vector.memset(minus_half[:], -0.5)
        gain = keep.tile([P, 1], F32)
        nc.vector.memset(gain[:], 1.0)

        g1_grouped = keep.tile([P, B, J, PACK], BF16, align_bytes=64)
        g1_codes = keep.tile([P, N_GROUPS, GROUP * J], U32, align_bytes=64)
        g1_scales = keep.tile([P, N_GROUPS, GROUP * J], U8, align_bytes=64)
        w_grouped = keep.tile([P, CHUNKS, K, P, PACK], BF16, align_bytes=64)
        w_codes = keep.tile([P, CHUNKS, K * P], U32, align_bytes=64)
        w_scales = keep.tile([P, CHUNKS, K * P], U8, align_bytes=64)
        a_grouped = keep.tile([P, B, J, PACK], BF16, align_bytes=64)
        a_codes = keep.tile([P, B, J], U32, align_bytes=64)
        a_scales = keep.tile([P, B, J], U8, align_bytes=64)

        def transpose_two(rows_0, rows_1, selector):
            bank = psum_tr.tile([P, 2, 2, P], F32, tag="bank")
            for i, rows in enumerate((rows_0, rows_1)):
                words = rows.bitcast(F32)
                for u in range(2):
                    nc.tensor.transpose(bank[:, i, u, :], words[:, u * P : (u + 1) * P], selector[:])
            return bank

        def group_two(on_scalar, grouped, bank):
            out_words = (
                grouped.rearrange("p i n e -> p (i n e)").bitcast(F32).rearrange("p (i n u) -> p i n u", i=2, u=2)
            )
            in_words = bank[:].rearrange("p i u n -> p i n u")
            if on_scalar:
                nc.scalar.copy(out=out_words, in_=in_words)
            else:
                nc.vector.tensor_copy(out=out_words, in_=in_words)

        def spread_g1(g):
            for pair in range(GROUP // 2):
                b = g * GROUP + 2 * pair
                bank = transpose_two(g1_sb[:, b, :], g1_sb[:, b + 1, :], joint_order)
                group_two(pair % 2 == 1, g1_grouped[:, b : b + 2], bank)

        def quantise_g1(g):
            nc.vector.quantize_mx(
                out=g1_codes[:, g, :].bitcast(FP8X4),
                scales=g1_scales[:, g, :],
                in_=g1_grouped[:, g * GROUP : (g + 1) * GROUP].rearrange("p b n e -> p (b n e)"),
            )

        def spread_w(q):
            for pair in range(K // 2):
                k = 2 * pair
                bank = transpose_two(w_sb[:, q, k, :], w_sb[:, q, k + 1, :], ident_f32)
                group_two(pair % 2 == 1, w_grouped[:, q, k : k + 2], bank)

        def quantise_w(q):
            nc.vector.quantize_mx(
                out=w_codes[:, q, :].bitcast(FP8X4),
                scales=w_scales[:, q, :],
                in_=w_grouped[:, q].rearrange("p k m e -> p (k m e)"),
            )

        def prepare_a():
            nc.vector.tensor_copy(out=gain[0:R, :], in_=s2_all[0:R, :])
            halves = [slice(half * B // 2, (half + 1) * B // 2) for half in range(2)]
            for samples in halves:
                nc.vector.tensor_scalar(
                    out=a_grouped[:, samples],
                    in0=a_raw[:, samples].rearrange("p b (t w) -> p b w t", t=PACK),
                    scalar1=gain[:, 0:1],
                    scalar2=None,
                    op0=ALU.mult,
                )
            for samples in halves:
                nc.vector.quantize_mx(
                    out=a_codes[:, samples, :].rearrange("p b w -> p (b w)").bitcast(FP8X4),
                    scales=a_scales[:, samples, :].rearrange("p b w -> p (b w)"),
                    in_=a_grouped[:, samples].rearrange("p b w t -> p (b w t)"),
                )

        h_t = {}

        def step1(g, q):
            if q == 0:
                h_t_new = per_group.tile([P, GROUP, CHUNKS, C], BF16, tag="h_t")
                h_t[g] = h_t_new
            for k in range(K):
                acc = psum_s1.tile([P, GROUP * J], F32)
                nc.tensor.matmul_mx(
                    out=acc[:],
                    lhsT=w_codes[:, q, k * P : (k + 1) * P].bitcast(FP8X4),
                    lhsT_scale=w_scales[:, q, k * P : (k + 1) * P],
                    rhs=g1_codes[:, g, :].bitcast(FP8X4),
                    rhs_scale=g1_scales[:, g, :],
                    start=True,
                    stop=True,
                )
                nc.scalar.activation(
                    out=h_t[g][:, :, q, :].rearrange("p b (a k n) -> p b a k n", a=2, k=K)[:, :, :, k, :],
                    in_=acc[:].rearrange("p (b a n) -> p b a n", b=GROUP, a=2),
                    func=ACT.Identity,
                    bias=bias_col[:, k * CHUNKS + q : k * CHUNKS + q + 1],
                    scale=1.0,
                )

        h_banks = {}
        h_grouped = {}
        g2 = {}
        x2 = {}
        stats = {}
        mean_var = {}
        rstd = {}
        centred = {}

        def transpose_h(b):
            rows = h_t[b // GROUP][:, b % GROUP]
            h_banks[b] = [transpose_two(rows[:, 2 * half, :], rows[:, 2 * half + 1, :], ident_f32) for half in range(2)]

        def group_h(b):
            h_grouped_new = per_sample.tile([P, CHUNKS, P, PACK], BF16, align_bytes=64, tag="h_grouped")
            h_grouped[b] = h_grouped_new
            for half in range(2):
                group_two(True, h_grouped_new[:, 2 * half : 2 * half + 2], h_banks[b][half])

        def step2(b):
            h_codes = per_sample.tile([P, C], U32, align_bytes=64)
            h_scales = per_sample.tile([P, C], U8, align_bytes=64)
            nc.vector.quantize_mx(
                out=h_codes[:].bitcast(FP8X4), scales=h_scales[:], in_=h_grouped[b][:].rearrange("p q c t -> p (q c t)")
            )
            g2_new = psum_s2.tile([P, C], F32, tag="g2")
            g2[b] = g2_new
            nc.tensor.matmul_mx(
                out=g2_new[:],
                lhsT=a_codes[:, b, :].bitcast(FP8X4),
                lhsT_scale=a_scales[:, b, :],
                rhs=h_codes[:].bitcast(FP8X4),
                rhs_scale=h_scales[:],
                start=True,
                stop=True,
            )

        def residual(b):
            x2_new = per_sample.tile([P, C], F32, tag="x2")
            x2[b] = x2_new
            nc.vector.tensor_tensor(out=x2_new[:], in0=g2[b][:], in1=res1_sb[:, b, :], op=ALU.add)
            nc.sync.dma_start(out=out_0[b], in_=x2_new[:])

        def statistics(b):
            stats_new = per_sample.tile([P, 6], F32, tag="stats")
            stats[b] = stats_new
            nc.vector.bn_stats(out=stats_new[:], in_=x2[b][:])

        def mean_and_rstd(b):
            mean_var_new = per_sample.tile([P, 2], F32, tag="mean_var")
            mean_var[b] = mean_var_new
            nc.vector.bn_aggr(out=mean_var_new[:], in_=stats[b][:])
            var_eps = per_sample.tile([P, 1], F32)
            nc.gpsimd.tensor_scalar(out=var_eps[:], in0=mean_var_new[:, 1:2], scalar1=EPS, scalar2=None, op0=ALU.add)
            rstd_new = per_sample.tile([P, 1], F32, tag="rstd")
            rstd[b] = rstd_new
            nc.gpsimd.tensor_tensor(out=rstd_new[:], in0=var_eps[:], in1=minus_half[:], op=ALU.pow)

        def centre(b):
            centred_new = per_sample.tile([P, C], F32, tag="centred")
            centred[b] = centred_new
            nc.vector.scalar_tensor_tensor(
                out=centred_new[:], in0=x2[b][:], scalar=mean_var[b][:, 0:1], in1=gamma[:], op0=ALU.subtract, op1=ALU.mult
            )

        def scale_and_shift(b):
            xn = per_sample.tile([P, C], F32)
            nc.vector.scalar_tensor_tensor(
                out=xn[:], in0=centred[b][:], scalar=rstd[b][:, 0:1], in1=beta[:], op0=ALU.mult, op1=ALU.add
            )
            nc.sync.dma_start(out=out_1[b], in_=xn[:])


        spread_g1(0)
        spread_w(0)
        quantise_g1(0)
        quantise_w(0)
        spread_w(1)
        bias_ps = psum_tr.tile([P, P], BF16, tag="bank")
        nc.tensor.transpose(bias_ps[:], bias_rows[:], ident_bf16[:])
        bias_col = keep.tile([P, K * CHUNKS], F32)
        nc.vector.tensor_copy(out=bias_col[:], in_=bias_ps[:, 0 : K * CHUNKS])
        for q in range(CHUNKS):
            if q + 1 < CHUNKS:
                quantise_w(q + 1)
            if q + 1 == CHUNKS:
                for g in range(1, N_GROUPS):
                    quantise_g1(g)
            step1(0, q)
            if q + 2 < CHUNKS:
                spread_w(q + 2)
            if q + 2 == CHUNKS:
                for g in range(1, N_GROUPS):
                    spread_g1(g)
        prepare_a()

        chunks_a_round = CHUNKS // GROUP
        transpose_h(0)
        for b in range(B + 2):
            if b < B:
                group_h(b)
                if b // GROUP + 1 < N_GROUPS:
                    for q in range((b % GROUP) * chunks_a_round, (b % GROUP + 1) * chunks_a_round):
                        step1(b // GROUP + 1, q)
                if b + 1 < B:
                    transpose_h(b + 1)
                step2(b)
            if 0 <= b - 1 < B:
                residual(b - 1)
            if 0 <= b - 2:
                centre(b - 2)
            if 0 <= b - 1 < B:
                statistics(b - 1)
            if 0 <= b - 2:
                scale_and_shift(b - 2)
            if 0 <= b - 1 < B:
                mean_and_rstd(b - 1)
